import numpy as np
import ml_dtypes


def mxq(x, axis, fmt="e4m3"):
    dtype, down = {"e4m3": (ml_dtypes.float8_e4m3fn, 7), "e5m2": (ml_dtypes.float8_e5m2, 14)}[fmt]
    v = np.moveaxis(np.asarray(x, np.float32).astype(ml_dtypes.bfloat16).astype(np.float64), axis, -1)
    blocks = v.reshape(v.shape[:-1] + (-1, 32))
    amax = np.abs(blocks).max(-1, keepdims=True)
    byte = np.maximum(np.where(amax > 0, np.frexp(amax)[1] - 1 + 127, 0) - down, 1)
    scale = np.exp2(byte - 127.0)
    codes = (blocks / scale).astype(np.float32).astype(dtype).astype(np.float64)
    return np.moveaxis((codes * scale).reshape(v.shape), -1, axis)


WIDE = False


def mx_kscale(k):
    if not WIDE:
        return np.ones(k)
    levels = np.array([10, -10, 5, -5, 0])
    a = np.random.permutation(np.resize(levels, k // 512 * 4)).reshape(k // 512, 4)
    idx = np.arange(k)
    return np.exp2(a[idx // 512, idx % 128 // 32])


BF16 = ml_dtypes.bfloat16


def bf(x):
    return np.asarray(x, np.float32).astype(BF16)


def f64(x):
    return np.asarray(x).astype(np.float64)


B, S, H, NH, NKV, HD = 2, 4096, 512, 2, 1, 128
ROPE_THETA = 10000.0


def rope_tables():
    inv_freq = 1.0 / (ROPE_THETA ** (np.arange(0, HD, 2) / HD))
    pos = np.arange(S)[None, :] + np.random.randint(0, S, (B, 1))
    freqs = pos[:, :, None] * inv_freq[None, None, :]
    emb = np.concatenate([freqs, freqs], axis=-1)
    return np.cos(emb), np.sin(emb)


def rotate_half(x):
    x1, x2 = np.split(x, 2, axis=-1)
    return np.concatenate([-x2, x1], axis=-1)


def setup_inputs():
    s = mx_kscale(H)
    hidden_states = bf(np.random.standard_normal((B, S, H)) * s)
    q_w = bf(np.random.standard_normal((NH * HD, H)) / np.sqrt(H) / s[None, :])
    k_w = bf(np.random.standard_normal((NKV * HD, H)) / np.sqrt(H) / s[None, :])
    v_w = bf(np.random.standard_normal((NKV * HD, H)) / np.sqrt(H) / s[None, :])
    cos, sin = rope_tables()
    return {"hidden_states": hidden_states, "cos": bf(cos), "sin": bf(sin), "q_w": q_w, "k_w": k_w, "v_w": v_w}


def reference(hidden_states, cos, sin, q_w, k_w, v_w):
    b, s, _ = hidden_states.shape
    xq = mxq(f64(hidden_states), 2, "e4m3")
    q = (xq @ mxq(f64(q_w), 1, "e4m3").T).reshape(b, s, NH, HD).transpose(0, 2, 1, 3)
    k = (xq @ mxq(f64(k_w), 1, "e4m3").T).reshape(b, s, NKV, HD).transpose(0, 2, 1, 3)
    v = (xq @ mxq(f64(v_w), 1, "e4m3").T).reshape(b, s, NKV, HD).transpose(0, 2, 1, 3)
    c = f64(cos)[:, None, :, :]
    sn = f64(sin)[:, None, :, :]
    q = q * c + rotate_half(q) * sn
    k = k * c + rotate_half(k) * sn
    return (q, k, v)

@@ -1,0 +1,213 @@
+from contextlib import ExitStack
+
+import concourse.mybir as mybir
+from concourse.masks import make_identity
+
+F32 = mybir.dt.float32
+BF16 = mybir.dt.bfloat16
+U32 = mybir.dt.uint32
+U8 = mybir.dt.uint8
+FP8X4 = mybir.dt.float8_e4m3fn_x4
+ALU = mybir.AluOpType
+
+P = 128
+B, S, H, HD = 2, 4096, 512, 128
+TPB = S // P
+GT = 4
+BT = 8
+NBLK = B * TPB // BT
+GPB = BT // GT
+NG = NBLK * GPB
+FLOPS = 2 * B * S * H * 512
+
+
+def tile_mistralattention_t_kernel(tc, hidden_states, cos, sin, q_w, k_w, v_w, out_0, out_1, out_2):
+    nc = tc.nc
+    with ExitStack() as ctx:
+        const = ctx.enter_context(tc.tile_pool(name="const", bufs=1))
+        xpool = ctx.enter_context(tc.tile_pool(name="xpool", bufs=5))
+        cspool = ctx.enter_context(tc.tile_pool(name="cspool", bufs=5))
+        snpool = ctx.enter_context(tc.tile_pool(name="snpool", bufs=3))
+        gpool = ctx.enter_context(tc.tile_pool(name="gpool", bufs=3))
+        qpool = ctx.enter_context(tc.tile_pool(name="qpool", bufs=3))
+        tpool = ctx.enter_context(tc.tile_pool(name="tpool", bufs=4))
+        ps_t = ctx.enter_context(tc.psum_pool(name="ps_t", bufs=2))
+        ps_y = ctx.enter_context(tc.psum_pool(name="ps_y", bufs=6))
+        ctx.enter_context(tc.manual_schedule())
+
+        ident = const.tile([P, P], F32)
+        make_identity(nc, ident[:])
+
+        w_sb = const.tile([P, 4 * H], BF16)
+        nc.sync.dma_start(
+            out=w_sb[:, 0 : 2 * H].rearrange("p (a k) -> p a k", a=2),
+            in_=q_w.rearrange("(a p) k -> p a k", p=P),
+        )
+        nc.sync.dma_start(out=w_sb[:, 2 * H : 3 * H], in_=k_w)
+        nc.sync.dma_start(out=w_sb[:, 3 * H : 4 * H], in_=v_w)
+
+        xs_blk = {}
+        cs_blk = {}
+        sn_blk = {}
+
+        def load_block(n):
+            b, t0 = divmod(n * BT, TPB)
+            xb = xpool.tile([P, BT * H], BF16, name="xb")
+            xv = hidden_states[b].rearrange("(p t) k -> p t k", t=TPB)
+            cs = cspool.tile([P, 2, BT, HD], BF16, name="cs")
+            sn = snpool.tile([P, BT, HD], BF16, name="sn")
+            pieces = GPB if n == 0 else 1
+            w = BT // pieces
+            for g in range(pieces):
+                nc.sync.dma_start(
+                    out=xb[:, g * w * H : (g + 1) * w * H],
+                    in_=xv[:, t0 + g * w : t0 + (g + 1) * w, :].rearrange("p t k -> p (t k)"),
+                )
+                if g == 0:
+                    nc.sync.dma_start(out=sn[:], in_=sin[b].rearrange("(p t) d -> p t d", t=TPB)[:, t0 : t0 + BT, :])
+                    nc.sync.dma_start(out=cs[:, 0], in_=cos[b].rearrange("(p t) d -> p t d", t=TPB)[:, t0 : t0 + BT, :])
+            xs_blk[n] = xb
+            cs_blk[n] = cs
+            sn_blk[n] = sn
+
+        def swap_sin(n):
+            cs, sn = cs_blk[n], sn_blk[n]
+            nc.scalar.copy(out=cs[:, 1, :, 0:64], in_=sn[:, :, 64:128])
+            nc.scalar.copy(out=cs[:, 1, :, 64:128], in_=sn[:, :, 0:64])
+
+        def transpose_group(src_words, on_vector):
+            grp = gpool.tile([P, GT * H], BF16, name="grp", align_bytes=64)
+            gw = grp[:].bitcast(F32)
+            for half in range(2):
+                xt = ps_t.tile([P, 512], F32, name="xt")
+                for j in range(4):
+                    c = half * 512 + j * 128
+                    nc.tensor.transpose(xt[:, j * 128 : (j + 1) * 128], src_words[:, c : c + 128], ident[:])
+                dst = gw[:, half * 512 : (half + 1) * 512].rearrange("p (a r u) -> p a r u", a=2, u=2)
+                src = xt[:].rearrange("p (a u r) -> p a r u", a=2, u=2)
+                if on_vector:
+                    nc.vector.tensor_copy(out=dst, in_=src)
+                else:
+                    nc.scalar.copy(out=dst, in_=src)
+            return grp
+
+        def quantise(grp, pool, name):
+            codes = pool.tile([P, GT * P], U32, name=name + "c", align_bytes=64)
+            scales = pool.tile([P, GT * P], U8, name=name + "s", align_bytes=64)
+            nc.vector.quantize_mx(out=codes[:].bitcast(FP8X4), scales=scales[:], in_=grp[:])
+            return codes, scales
+
+        grp_of = {}
+        q_of = {}
+
+        def prep(g):
+            n, gi = divmod(g, GPB)
+            xw = xs_blk[n][:].bitcast(F32)
+            grp_of[g] = transpose_group(xw[:, gi * GT * 256 : (gi + 1) * GT * 256], False)
+
+        def quant(g):
+            q_of[g] = quantise(grp_of[g], qpool, "x")
+
+        t_blk = {}
+        v_blk = {}
+
+        def combine(eng, g, h0, h1):
+            n, gi = divmod(g, GPB)
+            tt = t_blk[n]
+            t0 = gi * GT
+            lo = tt[:, 0, h0:h1, t0 : t0 + GT, 0:64]
+            hi = tt[:, 0, h0:h1, t0 : t0 + GT, 64:128]
+            eng.tensor_tensor(out=lo, in0=lo, in1=tt[:, 1, h0:h1, t0 : t0 + GT, 64:128], op=ALU.subtract)
+            eng.tensor_tensor(out=hi, in0=hi, in1=tt[:, 1, h0:h1, t0 : t0 + GT, 0:64], op=ALU.add)
+
+        def store(n, what, ta, tb):
+            b, t0 = divmod(n * BT, TPB)
+            tt, vo = t_blk[n], v_blk[n]
+            if what == "q":
+                nc.sync.dma_start(
+                    out=out_0[b].rearrange("h (p t) d -> p h t d", t=TPB)[:, :, t0 + ta : t0 + tb, :],
+                    in_=tt[:, 0, 0:2, ta:tb, :],
+                )
+            elif what == "k":
+                nc.sync.dma_start(
+                    out=out_1[b, 0].rearrange("(p t) d -> p t d", t=TPB)[:, t0 + ta : t0 + tb, :],
+                    in_=tt[:, 0, 2, ta:tb, :],
+                )
+            else:
+                nc.sync.dma_start(
+                    out=out_2[b, 0].rearrange("(p t) d -> p t d", t=TPB)[:, t0 + ta : t0 + tb, :], in_=vo[:, ta:tb, :]
+                )
+
+        def project(g):
+            n, gi = divmod(g, GPB)
+            last = g == NG - 1
+            if gi == 0:
+                t_blk[n] = tpool.tile([P, 2, 3, BT, HD], F32, name="tt")
+                v_blk[n] = tpool.tile([P, BT, HD], F32, name="vo")
+            tt, vo, cs = t_blk[n], v_blk[n], cs_blk[n]
+            xc, xs = q_of[g]
+            t0 = gi * GT
+            order = (3, 0, 1, 2) if last else (0, 1, 2, 3)
+            for hb in order:
+                y = ps_y.tile([P, 512], F32, name="y")
+                for j in range(GT):
+                    nc.tensor.matmul_mx(
+                        out=y[:, j * P : (j + 1) * P],
+                        lhsT=xc[:, j * P : (j + 1) * P].bitcast(FP8X4),
+                        lhsT_scale=xs[:, j * P : (j + 1) * P],
+                        rhs=wc[:, hb * P : (hb + 1) * P].bitcast(FP8X4),
+                        rhs_scale=ws[:, hb * P : (hb + 1) * P],
+                        start=True,
+                        stop=True,
+                    )
+                if hb < 3:
+                    nc.vector.tensor_tensor(
+                        out=tt[:, :, hb, t0 : t0 + GT, :].rearrange("p r t d -> p r (t d)"),
+                        in0=y[:].unsqueeze(1).to_broadcast([P, 2, 512]),
+                        in1=cs[:, :, t0 : t0 + GT, :].rearrange("p r t d -> p r (t d)"),
+                        op=ALU.mult,
+                    )
+                else:
+                    nc.scalar.copy(out=vo[:, t0 : t0 + GT, :].rearrange("p t d -> p (t d)"), in_=y[:])
+                if last and hb == 3:
+                    store(n, "v", t0, t0 + GT)
+                if last and hb == 1:
+                    combine(nc.vector, g, 0, 2)
+                    store(n, "q", t0, t0 + GT)
+                if last and hb == 2:
+                    combine(nc.vector, g, 2, 3)
+                    store(n, "k", t0, t0 + GT)
+
+        load_block(0)
+        wgrp = transpose_group(w_sb[:].bitcast(F32), True)
+        prep(0)
+        wc, ws = quantise(wgrp, const, "w")
+        load_block(1)
+        quant(0)
+        swap_sin(0)
+        load_block(2)
+        prep(1)
+        quant(1)
+        prep(2)
+        load_block(3)
+        load_block(4)
+        for g in range(NG):
+            n, gi = divmod(g, GPB)
+            if gi == 0 and n + 1 < NBLK:
+                swap_sin(n + 1)
+            if g + 3 < NG:
+                prep(g + 3)
+            if g + 2 < NG:
+                quant(g + 2)
+            project(g)
+            if gi == 0 and 5 <= n + 4 < NBLK:
+                load_block(n + 4)
+            if g < NG - 1:
+                combine(nc.gpsimd, g, 0, 3)
+            if n < NBLK - 1:
+                if gi == GPB - 1:
+                    for what in ("q", "k", "v"):
+                        store(n, what, 0, BT)
+            elif g < NG - 1:
+                for what in ("q", "k", "v"):
+                    store(n, what, gi * GT, (gi + 1) * GT)

@@ -18,6 +18,8 @@ BT = 8
 NBLK = B * TPB // BT
 GPB = BT // GT
 NG = NBLK * GPB
+XBUFS = 6
+FINE = 2
 FLOPS = 2 * B * S * H * 512
 
 
@@ -25,9 +27,9 @@ def tile_mistralattention_t_kernel(tc, hidden_states, cos, sin, q_w, k_w, v_w, o
     nc = tc.nc
     with ExitStack() as ctx:
         const = ctx.enter_context(tc.tile_pool(name="const", bufs=1))
-        xpool = ctx.enter_context(tc.tile_pool(name="xpool", bufs=5))
-        cspool = ctx.enter_context(tc.tile_pool(name="cspool", bufs=5))
-        snpool = ctx.enter_context(tc.tile_pool(name="snpool", bufs=3))
+        xpool = ctx.enter_context(tc.tile_pool(name="xpool", bufs=XBUFS))
+        cspool = ctx.enter_context(tc.tile_pool(name="cspool", bufs=XBUFS))
+        snpool = ctx.enter_context(tc.tile_pool(name="snpool", bufs=6))
         gpool = ctx.enter_context(tc.tile_pool(name="gpool", bufs=3))
         qpool = ctx.enter_context(tc.tile_pool(name="qpool", bufs=3))
         tpool = ctx.enter_context(tc.tile_pool(name="tpool", bufs=4))
@@ -39,74 +41,85 @@ def tile_mistralattention_t_kernel(tc, hidden_states, cos, sin, q_w, k_w, v_w, o
         make_identity(nc, ident[:])
 
         w_sb = const.tile([P, 4 * H], BF16)
-        nc.sync.dma_start(
-            out=w_sb[:, 0 : 2 * H].rearrange("p (a k) -> p a k", a=2),
-            in_=q_w.rearrange("(a p) k -> p a k", p=P),
-        )
-        nc.sync.dma_start(out=w_sb[:, 2 * H : 3 * H], in_=k_w)
-        nc.sync.dma_start(out=w_sb[:, 3 * H : 4 * H], in_=v_w)
+        wgrp = const.tile([P, 4 * H], BF16, align_bytes=64)
+        wc = const.tile([P, 4 * P], U32, align_bytes=64)
+        ws = const.tile([P, 4 * P], U8, align_bytes=64)
 
         xs_blk = {}
         cs_blk = {}
         sn_blk = {}
 
-        def load_block(n):
+        def new_block(n):
+            xs_blk[n] = xpool.tile([P, BT * H], BF16, name="xb")
+            cs_blk[n] = cspool.tile([P, 2, BT, HD], BF16, name="cs")
+            sn_blk[n] = snpool.tile([P, BT, HD], BF16, name="sn")
+
+        def load_x(n, ta, tb):
             b, t0 = divmod(n * BT, TPB)
-            xb = xpool.tile([P, BT * H], BF16, name="xb")
             xv = hidden_states[b].rearrange("(p t) k -> p t k", t=TPB)
-            cs = cspool.tile([P, 2, BT, HD], BF16, name="cs")
-            sn = snpool.tile([P, BT, HD], BF16, name="sn")
-            pieces = GPB if n == 0 else 1
-            w = BT // pieces
-            for g in range(pieces):
-                nc.sync.dma_start(
-                    out=xb[:, g * w * H : (g + 1) * w * H],
-                    in_=xv[:, t0 + g * w : t0 + (g + 1) * w, :].rearrange("p t k -> p (t k)"),
-                )
-                if g == 0:
-                    nc.sync.dma_start(out=sn[:], in_=sin[b].rearrange("(p t) d -> p t d", t=TPB)[:, t0 : t0 + BT, :])
-                    nc.sync.dma_start(out=cs[:, 0], in_=cos[b].rearrange("(p t) d -> p t d", t=TPB)[:, t0 : t0 + BT, :])
-            xs_blk[n] = xb
-            cs_blk[n] = cs
-            sn_blk[n] = sn
+            nc.sync.dma_start(
+                out=xs_blk[n][:, ta * H : tb * H], in_=xv[:, t0 + ta : t0 + tb, :].rearrange("p t k -> p (t k)")
+            )
 
-        def swap_sin(n):
+        def load_tables(n):
+            b, t0 = divmod(n * BT, TPB)
+            nc.sync.dma_start(out=sn_blk[n][:], in_=sin[b].rearrange("(p t) d -> p t d", t=TPB)[:, t0 : t0 + BT, :])
+            nc.sync.dma_start(
+                out=cs_blk[n][:, 0], in_=cos[b].rearrange("(p t) d -> p t d", t=TPB)[:, t0 : t0 + BT, :]
+            )
+
+        def load_block(n):
+            new_block(n)
+            load_x(n, 0, BT)
+            load_tables(n)
+
+        def swap_sin(n, on_vector):
             cs, sn = cs_blk[n], sn_blk[n]
-            nc.scalar.copy(out=cs[:, 1, :, 0:64], in_=sn[:, :, 64:128])
-            nc.scalar.copy(out=cs[:, 1, :, 64:128], in_=sn[:, :, 0:64])
-
-        def transpose_group(src_words, on_vector):
-            grp = gpool.tile([P, GT * H], BF16, name="grp", align_bytes=64)
-            gw = grp[:].bitcast(F32)
-            for half in range(2):
-                xt = ps_t.tile([P, 512], F32, name="xt")
-                for j in range(4):
-                    c = half * 512 + j * 128
-                    nc.tensor.transpose(xt[:, j * 128 : (j + 1) * 128], src_words[:, c : c + 128], ident[:])
-                dst = gw[:, half * 512 : (half + 1) * 512].rearrange("p (a r u) -> p a r u", a=2, u=2)
-                src = xt[:].rearrange("p (a u r) -> p a r u", a=2, u=2)
+            for a, b in ((0, 64), (64, 0)):
                 if on_vector:
-                    nc.vector.tensor_copy(out=dst, in_=src)
+                    nc.vector.tensor_copy(out=cs[:, 1, :, a : a + 64], in_=sn[:, :, b : b + 64])
                 else:
-                    nc.scalar.copy(out=dst, in_=src)
-            return grp
+                    nc.scalar.copy(out=cs[:, 1, :, a : a + 64], in_=sn[:, :, b : b + 64])
 
-        def quantise(grp, pool, name):
-            codes = pool.tile([P, GT * P], U32, name=name + "c", align_bytes=64)
-            scales = pool.tile([P, GT * P], U8, name=name + "s", align_bytes=64)
-            nc.vector.quantize_mx(out=codes[:].bitcast(FP8X4), scales=scales[:], in_=grp[:])
-            return codes, scales
+        def transpose_pair(src_words, dst_words, on_vector):
+            xt = ps_t.tile([P, 512], F32, name="xt")
+            for j in range(4):
+                nc.tensor.transpose(xt[:, j * 128 : (j + 1) * 128], src_words[:, j * 128 : (j + 1) * 128], ident[:])
+            dst = dst_words.rearrange("p (a r u) -> p a r u", a=2, u=2)
+            src = xt[:].rearrange("p (a u r) -> p a r u", a=2, u=2)
+            if on_vector:
+                nc.vector.tensor_copy(out=dst, in_=src)
+            else:
+                nc.scalar.copy(out=dst, in_=src)
+
+        def quantise(grp, codes, scales, c0, c1):
+            nc.vector.quantize_mx(
+                out=codes[:, c0:c1].bitcast(FP8X4), scales=scales[:, c0:c1], in_=grp[:, 4 * c0 : 4 * c1]
+            )
 
         grp_of = {}
         q_of = {}
 
-        def prep(g):
+        def prep_half(g, half):
             n, gi = divmod(g, GPB)
+            if half == 0:
+                grp_of[g] = gpool.tile([P, GT * H], BF16, name="grp", align_bytes=64)
             xw = xs_blk[n][:].bitcast(F32)
-            grp_of[g] = transpose_group(xw[:, gi * GT * 256 : (gi + 1) * GT * 256], False)
+            c = gi * GT * 256 + half * 512
+            transpose_pair(xw[:, c : c + 512], grp_of[g][:].bitcast(F32)[:, half * 512 : (half + 1) * 512], False)
+
+        def prep(g):
+            prep_half(g, 0)
+            prep_half(g, 1)
+
+        def new_codes(g):
+            xc = qpool.tile([P, GT * P], U32, name="xc", align_bytes=64)
+            xs = qpool.tile([P, GT * P], U8, name="xs", align_bytes=64)
+            q_of[g] = (xc, xs)
 
         def quant(g):
-            q_of[g] = quantise(grp_of[g], qpool, "x")
+            new_codes(g)
+            quantise(grp_of[g], q_of[g][0], q_of[g][1], 0, GT * P)
 
         t_blk = {}
         v_blk = {}
@@ -138,76 +151,99 @@ def tile_mistralattention_t_kernel(tc, hidden_states, cos, sin, q_w, k_w, v_w, o
                     out=out_2[b, 0].rearrange("(p t) d -> p t d", t=TPB)[:, t0 + ta : t0 + tb, :], in_=vo[:, ta:tb, :]
                 )
 
-        def project(g):
+        def passes(g, hb):
+            xc, xs = q_of[g]
+            y = ps_y.tile([P, 512], F32, name="y")
+            for j in range(GT):
+                nc.tensor.matmul_mx(
+                    out=y[:, j * P : (j + 1) * P],
+                    lhsT=xc[:, j * P : (j + 1) * P].bitcast(FP8X4),
+                    lhsT_scale=xs[:, j * P : (j + 1) * P],
+                    rhs=wc[:, hb * P : (hb + 1) * P].bitcast(FP8X4),
+                    rhs_scale=ws[:, hb * P : (hb + 1) * P],
+                    start=True,
+                    stop=True,
+                )
+            return y
+
+        def head(g, hb):
             n, gi = divmod(g, GPB)
-            last = g == NG - 1
-            if gi == 0:
+            if n not in t_blk:
                 t_blk[n] = tpool.tile([P, 2, 3, BT, HD], F32, name="tt")
                 v_blk[n] = tpool.tile([P, BT, HD], F32, name="vo")
             tt, vo, cs = t_blk[n], v_blk[n], cs_blk[n]
-            xc, xs = q_of[g]
             t0 = gi * GT
-            order = (3, 0, 1, 2) if last else (0, 1, 2, 3)
-            for hb in order:
-                y = ps_y.tile([P, 512], F32, name="y")
-                for j in range(GT):
-                    nc.tensor.matmul_mx(
-                        out=y[:, j * P : (j + 1) * P],
-                        lhsT=xc[:, j * P : (j + 1) * P].bitcast(FP8X4),
-                        lhsT_scale=xs[:, j * P : (j + 1) * P],
-                        rhs=wc[:, hb * P : (hb + 1) * P].bitcast(FP8X4),
-                        rhs_scale=ws[:, hb * P : (hb + 1) * P],
-                        start=True,
-                        stop=True,
-                    )
-                if hb < 3:
-                    nc.vector.tensor_tensor(
-                        out=tt[:, :, hb, t0 : t0 + GT, :].rearrange("p r t d -> p r (t d)"),
-                        in0=y[:].unsqueeze(1).to_broadcast([P, 2, 512]),
-                        in1=cs[:, :, t0 : t0 + GT, :].rearrange("p r t d -> p r (t d)"),
-                        op=ALU.mult,
-                    )
-                else:
-                    nc.scalar.copy(out=vo[:, t0 : t0 + GT, :].rearrange("p t d -> p (t d)"), in_=y[:])
-                if last and hb == 3:
-                    store(n, "v", t0, t0 + GT)
-                if last and hb == 1:
-                    combine(nc.vector, g, 0, 2)
-                    store(n, "q", t0, t0 + GT)
-                if last and hb == 2:
-                    combine(nc.vector, g, 2, 3)
-                    store(n, "k", t0, t0 + GT)
+            y = passes(g, hb)
+            if hb < 3:
+                nc.vector.tensor_tensor(
+                    out=tt[:, :, hb, t0 : t0 + GT, :].rearrange("p r t d -> p r (t d)"),
+                    in0=y[:].unsqueeze(1).to_broadcast([P, 2, 512]),
+                    in1=cs[:, :, t0 : t0 + GT, :].rearrange("p r t d -> p r (t d)"),
+                    op=ALU.mult,
+                )
+            else:
+                nc.scalar.copy(out=vo[:, t0 : t0 + GT, :].rearrange("p t d -> p (t d)"), in_=y[:])
 
-        load_block(0)
-        wgrp = transpose_group(w_sb[:].bitcast(F32), True)
-        prep(0)
-        wc, ws = quantise(wgrp, const, "w")
-        load_block(1)
-        quant(0)
-        swap_sin(0)
-        load_block(2)
-        prep(1)
-        quant(1)
-        prep(2)
-        load_block(3)
-        load_block(4)
-        for g in range(NG):
+        ww = w_sb[:].bitcast(F32)
+        wgw = wgrp[:].bitcast(F32)
+        new_block(0)
+        nc.sync.dma_start(
+            out=w_sb[:, 0 : 2 * H].rearrange("p (a k) -> p a k", a=2), in_=q_w.rearrange("(a p) k -> p a k", p=P)
+        )
+        load_x(0, 0, 2)
+        load_x(0, 2, 4)
+        load_tables(0)
+        nc.sync.dma_start(out=w_sb[:, 2 * H : 3 * H], in_=k_w)
+        nc.sync.dma_start(out=w_sb[:, 3 * H : 4 * H], in_=v_w)
+        load_x(0, 4, 8)
+        for n in range(1, XBUFS):
+            load_block(n)
+
+        transpose_pair(ww[:, 0:512], wgw[:, 0:512], True)
+        prep_half(0, 0)
+        prep_half(0, 1)
+        transpose_pair(ww[:, 512:1024], wgw[:, 512:1024], False)
+        new_codes(0)
+        quantise(wgrp, wc, ws, 0, 256)
+        quantise(grp_of[0], q_of[0][0], q_of[0][1], 0, 256)
+        swap_sin(0, True)
+        quantise(grp_of[0], q_of[0][0], q_of[0][1], 256, 512)
+
+        for g in range(NG - 1):
             n, gi = divmod(g, GPB)
+            head(g, 0)
+            if g == 0:
+                quantise(wgrp, wc, ws, 256, 512)
+            if g >= 2:
+                quant(g + 1)
+            head(g, 1)
+            if g < 2:
+                prep(g + 1)
+                quant(g + 1)
+            head(g, 2)
+            head(g, 3)
+            if g >= 1 and g + 2 < NG:
+                prep(g + 2)
             if gi == 0 and n + 1 < NBLK:
-                swap_sin(n + 1)
-            if g + 3 < NG:
-                prep(g + 3)
-            if g + 2 < NG:
-                quant(g + 2)
-            project(g)
-            if gi == 0 and 5 <= n + 4 < NBLK:
-                load_block(n + 4)
-            if g < NG - 1:
-                combine(nc.gpsimd, g, 0, 3)
-            if n < NBLK - 1:
-                if gi == GPB - 1:
-                    for what in ("q", "k", "v"):
-                        store(n, what, 0, BT)
-            elif g < NG - 1:
-                for what in ("q", "k", "v"):
+                swap_sin(n + 1, False)
+            combine(nc.gpsimd, g, 0, 3)
+            if n >= NBLK - FINE:
+                for what in ("v", "q", "k"):
                     store(n, what, gi * GT, (gi + 1) * GT)
+            elif gi == GPB - 1:
+                for what in ("v", "q", "k"):
+                    store(n, what, 0, BT)
+                if n + XBUFS < NBLK:
+                    load_block(n + XBUFS)
+
+        g = NG - 1
+        n, gi = divmod(g, GPB)
+        head(g, 3)
+        store(n, "v", gi * GT, (gi + 1) * GT)
+        head(g, 0)
+        head(g, 1)
+        combine(nc.vector, g, 0, 2)
+        store(n, "q", gi * GT, (gi + 1) * GT)
+        head(g, 2)
+        combine(nc.vector, g, 2, 3)
+        store(n, "k", gi * GT, (gi + 1) * GT)

@@ -196,7 +196,11 @@ def tile_mistralattention_t_kernel(tc, hidden_states, cos, sin, q_w, k_w, v_w, o
         nc.sync.dma_start(out=w_sb[:, 2 * H : 3 * H], in_=k_w)
         nc.sync.dma_start(out=w_sb[:, 3 * H : 4 * H], in_=v_w)
         load_x(0, 4, 8)
-        for n in range(1, XBUFS):
+        new_block(1)
+        load_x(1, 0, 4)
+        load_x(1, 4, 8)
+        load_tables(1)
+        for n in range(2, XBUFS):
             load_block(n)
 
         transpose_pair(ww[:, 0:512], wgw[:, 0:512], True)
@@ -214,16 +218,15 @@ def tile_mistralattention_t_kernel(tc, hidden_states, cos, sin, q_w, k_w, v_w, o
             head(g, 0)
             if g == 0:
                 quantise(wgrp, wc, ws, 256, 512)
-            if g >= 2:
-                quant(g + 1)
             head(g, 1)
-            if g < 2:
-                prep(g + 1)
-                quant(g + 1)
+            if g == 0:
+                prep(1)
+                quant(1)
             head(g, 2)
             head(g, 3)
-            if g >= 1 and g + 2 < NG:
+            if g + 2 < NG:
                 prep(g + 2)
+                quant(g + 2)
             if gi == 0 and n + 1 < NBLK:
                 swap_sin(n + 1, False)
             combine(nc.gpsimd, g, 0, 3)

@@ -19,7 +19,6 @@ NBLK = B * TPB // BT
 GPB = BT // GT
 NG = NBLK * GPB
 XBUFS = 6
-FINE = 2
 FLOPS = 2 * B * S * H * 512
 
 
@@ -32,7 +31,7 @@ def tile_mistralattention_t_kernel(tc, hidden_states, cos, sin, q_w, k_w, v_w, o
         snpool = ctx.enter_context(tc.tile_pool(name="snpool", bufs=6))
         gpool = ctx.enter_context(tc.tile_pool(name="gpool", bufs=3))
         qpool = ctx.enter_context(tc.tile_pool(name="qpool", bufs=3))
-        tpool = ctx.enter_context(tc.tile_pool(name="tpool", bufs=4))
+        tpool = ctx.enter_context(tc.tile_pool(name="tpool", bufs=8))
         ps_t = ctx.enter_context(tc.psum_pool(name="ps_t", bufs=2))
         ps_y = ctx.enter_context(tc.psum_pool(name="ps_y", bufs=6))
         ctx.enter_context(tc.manual_schedule())
@@ -75,11 +74,12 @@ def tile_mistralattention_t_kernel(tc, hidden_states, cos, sin, q_w, k_w, v_w, o
 
         def swap_sin(n, on_vector):
             cs, sn = cs_blk[n], sn_blk[n]
-            for a, b in ((0, 64), (64, 0)):
-                if on_vector:
-                    nc.vector.tensor_copy(out=cs[:, 1, :, a : a + 64], in_=sn[:, :, b : b + 64])
-                else:
-                    nc.scalar.copy(out=cs[:, 1, :, a : a + 64], in_=sn[:, :, b : b + 64])
+            if on_vector:
+                nc.vector.tensor_copy(out=cs[:, 1, :, 0:64], in_=sn[:, :, 64:128])
+                nc.vector.tensor_scalar_mul(out=cs[:, 1, :, 64:128], in0=sn[:, :, 0:64], scalar1=-1.0)
+            else:
+                nc.scalar.copy(out=cs[:, 1, :, 0:64], in_=sn[:, :, 64:128])
+                nc.scalar.mul(out=cs[:, 1, :, 64:128], in_=sn[:, :, 0:64], mul=-1.0)
 
         def transpose_pair(src_words, dst_words, on_vector):
             xt = ps_t.tile([P, 512], F32, name="xt")
@@ -125,31 +125,24 @@ def tile_mistralattention_t_kernel(tc, hidden_states, cos, sin, q_w, k_w, v_w, o
         v_blk = {}
 
         def combine(eng, g, h0, h1):
-            n, gi = divmod(g, GPB)
-            tt = t_blk[n]
-            t0 = gi * GT
-            lo = tt[:, 0, h0:h1, t0 : t0 + GT, 0:64]
-            hi = tt[:, 0, h0:h1, t0 : t0 + GT, 64:128]
-            eng.tensor_tensor(out=lo, in0=lo, in1=tt[:, 1, h0:h1, t0 : t0 + GT, 64:128], op=ALU.subtract)
-            eng.tensor_tensor(out=hi, in0=hi, in1=tt[:, 1, h0:h1, t0 : t0 + GT, 0:64], op=ALU.add)
+            tt = t_blk[g]
+            res = tt[:, 0, h0:h1, :, :].rearrange("p h t (f j) -> p (h t) f j", f=2)
+            oth = tt[:, 1, h0:h1, :, :].rearrange("p h t (f j) -> p (h t) f j", f=2)
+            eng.tensor_tensor(out=res, in0=res, in1=oth[:, :, ::-1, :], op=ALU.add)
 
-        def store(n, what, ta, tb):
-            b, t0 = divmod(n * BT, TPB)
-            tt, vo = t_blk[n], v_blk[n]
+        def store(g, what):
+            b, t0 = divmod(g * GT, TPB)
+            tt, vo = t_blk[g], v_blk[g]
             if what == "q":
                 nc.sync.dma_start(
-                    out=out_0[b].rearrange("h (p t) d -> p h t d", t=TPB)[:, :, t0 + ta : t0 + tb, :],
-                    in_=tt[:, 0, 0:2, ta:tb, :],
+                    out=out_0[b].rearrange("h (p t) d -> p h t d", t=TPB)[:, :, t0 : t0 + GT, :], in_=tt[:, 0, 0:2, :, :]
                 )
             elif what == "k":
                 nc.sync.dma_start(
-                    out=out_1[b, 0].rearrange("(p t) d -> p t d", t=TPB)[:, t0 + ta : t0 + tb, :],
-                    in_=tt[:, 0, 2, ta:tb, :],
+                    out=out_1[b, 0].rearrange("(p t) d -> p t d", t=TPB)[:, t0 : t0 + GT, :], in_=tt[:, 0, 2, :, :]
                 )
             else:
-                nc.sync.dma_start(
-                    out=out_2[b, 0].rearrange("(p t) d -> p t d", t=TPB)[:, t0 + ta : t0 + tb, :], in_=vo[:, ta:tb, :]
-                )
+                nc.sync.dma_start(out=out_2[b, 0].rearrange("(p t) d -> p t d", t=TPB)[:, t0 : t0 + GT, :], in_=vo[:])
 
         def passes(g, hb):
             xc, xs = q_of[g]
@@ -168,21 +161,21 @@ def tile_mistralattention_t_kernel(tc, hidden_states, cos, sin, q_w, k_w, v_w, o
 
         def head(g, hb):
             n, gi = divmod(g, GPB)
-            if n not in t_blk:
-                t_blk[n] = tpool.tile([P, 2, 3, BT, HD], F32, name="tt")
-                v_blk[n] = tpool.tile([P, BT, HD], F32, name="vo")
-            tt, vo, cs = t_blk[n], v_blk[n], cs_blk[n]
+            if g not in t_blk:
+                t_blk[g] = tpool.tile([P, 2, 3, GT, HD], F32, name="tt")
+                v_blk[g] = tpool.tile([P, GT, HD], F32, name="vo")
+            tt, vo, cs = t_blk[g], v_blk[g], cs_blk[n]
             t0 = gi * GT
             y = passes(g, hb)
             if hb < 3:
                 nc.vector.tensor_tensor(
-                    out=tt[:, :, hb, t0 : t0 + GT, :].rearrange("p r t d -> p r (t d)"),
+                    out=tt[:, :, hb, :, :].rearrange("p r t d -> p r (t d)"),
                     in0=y[:].unsqueeze(1).to_broadcast([P, 2, 512]),
                     in1=cs[:, :, t0 : t0 + GT, :].rearrange("p r t d -> p r (t d)"),
                     op=ALU.mult,
                 )
             else:
-                nc.scalar.copy(out=vo[:, t0 : t0 + GT, :].rearrange("p t d -> p (t d)"), in_=y[:])
+                nc.scalar.copy(out=vo[:].rearrange("p t d -> p (t d)"), in_=y[:])
 
         ww = w_sb[:].bitcast(F32)
         wgw = wgrp[:].bitcast(F32)
@@ -230,23 +223,18 @@ def tile_mistralattention_t_kernel(tc, hidden_states, cos, sin, q_w, k_w, v_w, o
             if gi == 0 and n + 1 < NBLK:
                 swap_sin(n + 1, False)
             combine(nc.gpsimd, g, 0, 3)
-            if n >= NBLK - FINE:
-                for what in ("v", "q", "k"):
-                    store(n, what, gi * GT, (gi + 1) * GT)
-            elif gi == GPB - 1:
-                for what in ("v", "q", "k"):
-                    store(n, what, 0, BT)
-                if n + XBUFS < NBLK:
-                    load_block(n + XBUFS)
+            for what in ("v", "q", "k"):
+                store(g, what)
+            if gi == GPB - 1 and n + XBUFS < NBLK:
+                load_block(n + XBUFS)
 
         g = NG - 1
-        n, gi = divmod(g, GPB)
         head(g, 3)
-        store(n, "v", gi * GT, (gi + 1) * GT)
+        store(g, "v")
         head(g, 0)
         head(g, 1)
         combine(nc.vector, g, 0, 2)
-        store(n, "q", gi * GT, (gi + 1) * GT)
+        store(g, "q")
         head(g, 2)
         combine(nc.vector, g, 2, 3)
-        store(n, "k", gi * GT, (gi + 1) * GT)
+        store(g, "k")

@@ -60,11 +60,13 @@ def tile_mistralattention_t_kernel(tc, hidden_states, cos, sin, q_w, k_w, v_w, o
                 out=xs_blk[n][:, ta * H : tb * H], in_=xv[:, t0 + ta : t0 + tb, :].rearrange("p t k -> p (t k)")
             )
 
-        def load_tables(n):
+        def load_tables(n, ta=0, tb=BT):
             b, t0 = divmod(n * BT, TPB)
-            nc.sync.dma_start(out=sn_blk[n][:], in_=sin[b].rearrange("(p t) d -> p t d", t=TPB)[:, t0 : t0 + BT, :])
             nc.sync.dma_start(
-                out=cs_blk[n][:, 0], in_=cos[b].rearrange("(p t) d -> p t d", t=TPB)[:, t0 : t0 + BT, :]
+                out=sn_blk[n][:, ta:tb, :], in_=sin[b].rearrange("(p t) d -> p t d", t=TPB)[:, t0 + ta : t0 + tb, :]
+            )
+            nc.sync.dma_start(
+                out=cs_blk[n][:, 0, ta:tb, :], in_=cos[b].rearrange("(p t) d -> p t d", t=TPB)[:, t0 + ta : t0 + tb, :]
             )
 
         def load_block(n):
@@ -72,14 +74,14 @@ def tile_mistralattention_t_kernel(tc, hidden_states, cos, sin, q_w, k_w, v_w, o
             load_x(n, 0, BT)
             load_tables(n)
 
-        def swap_sin(n, on_vector):
+        def swap_sin(n, on_vector, ta=0, tb=BT):
             cs, sn = cs_blk[n], sn_blk[n]
             if on_vector:
-                nc.vector.tensor_copy(out=cs[:, 1, :, 0:64], in_=sn[:, :, 64:128])
-                nc.vector.tensor_scalar_mul(out=cs[:, 1, :, 64:128], in0=sn[:, :, 0:64], scalar1=-1.0)
+                nc.vector.tensor_copy(out=cs[:, 1, ta:tb, 0:64], in_=sn[:, ta:tb, 64:128])
+                nc.vector.tensor_scalar_mul(out=cs[:, 1, ta:tb, 64:128], in0=sn[:, ta:tb, 0:64], scalar1=-1.0)
             else:
-                nc.scalar.copy(out=cs[:, 1, :, 0:64], in_=sn[:, :, 64:128])
-                nc.scalar.mul(out=cs[:, 1, :, 64:128], in_=sn[:, :, 0:64], mul=-1.0)
+                nc.scalar.copy(out=cs[:, 1, ta:tb, 0:64], in_=sn[:, ta:tb, 64:128])
+                nc.scalar.mul(out=cs[:, 1, ta:tb, 64:128], in_=sn[:, ta:tb, 0:64], mul=-1.0)
 
         def transpose_pair(src_words, dst_words, on_vector):
             xt = ps_t.tile([P, 512], F32, name="xt")
@@ -185,10 +187,11 @@ def tile_mistralattention_t_kernel(tc, hidden_states, cos, sin, q_w, k_w, v_w, o
         )
         load_x(0, 0, 2)
         load_x(0, 2, 4)
-        load_tables(0)
+        load_tables(0, 0, GT)
         nc.sync.dma_start(out=w_sb[:, 2 * H : 3 * H], in_=k_w)
         nc.sync.dma_start(out=w_sb[:, 3 * H : 4 * H], in_=v_w)
         load_x(0, 4, 8)
+        load_tables(0, GT, BT)
         new_block(1)
         load_x(1, 0, 4)
         load_x(1, 4, 8)
@@ -203,7 +206,7 @@ def tile_mistralattention_t_kernel(tc, hidden_states, cos, sin, q_w, k_w, v_w, o
         new_codes(0)
         quantise(wgrp, wc, ws, 0, 256)
         quantise(grp_of[0], q_of[0][0], q_of[0][1], 0, 256)
-        swap_sin(0, True)
+        swap_sin(0, True, 0, GT)
         quantise(grp_of[0], q_of[0][0], q_of[0][1], 256, 512)
 
         for g in range(NG - 1):
@@ -214,6 +217,7 @@ def tile_mistralattention_t_kernel(tc, hidden_states, cos, sin, q_w, k_w, v_w, o
             head(g, 1)
             if g == 0:
                 prep(1)
+                swap_sin(0, False, GT, BT)
                 quant(1)
             head(g, 2)
             head(g, 3)
@@ -233,8 +237,8 @@ def tile_mistralattention_t_kernel(tc, hidden_states, cos, sin, q_w, k_w, v_w, o
         store(g, "v")
         head(g, 0)
         head(g, 1)
+        head(g, 2)
         combine(nc.vector, g, 0, 2)
         store(g, "q")
-        head(g, 2)
         combine(nc.vector, g, 2, 3)
         store(g, "k")

@@ -34,7 +34,6 @@ def tile_mistralattention_t_kernel(tc, hidden_states, cos, sin, q_w, k_w, v_w, o
         tpool = ctx.enter_context(tc.tile_pool(name="tpool", bufs=8))
         ps_t = ctx.enter_context(tc.psum_pool(name="ps_t", bufs=2))
         ps_y = ctx.enter_context(tc.psum_pool(name="ps_y", bufs=6))
-        ctx.enter_context(tc.manual_schedule())
 
         ident = const.tile([P, P], F32)
         make_identity(nc, ident[:])
@@ -60,13 +59,11 @@ def tile_mistralattention_t_kernel(tc, hidden_states, cos, sin, q_w, k_w, v_w, o
                 out=xs_blk[n][:, ta * H : tb * H], in_=xv[:, t0 + ta : t0 + tb, :].rearrange("p t k -> p (t k)")
             )
 
-        def load_tables(n, ta=0, tb=BT):
+        def load_tables(n):
             b, t0 = divmod(n * BT, TPB)
+            nc.sync.dma_start(out=sn_blk[n][:], in_=sin[b].rearrange("(p t) d -> p t d", t=TPB)[:, t0 : t0 + BT, :])
             nc.sync.dma_start(
-                out=sn_blk[n][:, ta:tb, :], in_=sin[b].rearrange("(p t) d -> p t d", t=TPB)[:, t0 + ta : t0 + tb, :]
-            )
-            nc.sync.dma_start(
-                out=cs_blk[n][:, 0, ta:tb, :], in_=cos[b].rearrange("(p t) d -> p t d", t=TPB)[:, t0 + ta : t0 + tb, :]
+                out=cs_blk[n][:, 0], in_=cos[b].rearrange("(p t) d -> p t d", t=TPB)[:, t0 : t0 + BT, :]
             )
 
         def load_block(n):
@@ -74,14 +71,14 @@ def tile_mistralattention_t_kernel(tc, hidden_states, cos, sin, q_w, k_w, v_w, o
             load_x(n, 0, BT)
             load_tables(n)
 
-        def swap_sin(n, on_vector, ta=0, tb=BT):
+        def swap_sin(n, on_vector):
             cs, sn = cs_blk[n], sn_blk[n]
             if on_vector:
-                nc.vector.tensor_copy(out=cs[:, 1, ta:tb, 0:64], in_=sn[:, ta:tb, 64:128])
-                nc.vector.tensor_scalar_mul(out=cs[:, 1, ta:tb, 64:128], in0=sn[:, ta:tb, 0:64], scalar1=-1.0)
+                nc.vector.tensor_copy(out=cs[:, 1, :, 0:64], in_=sn[:, :, 64:128])
+                nc.vector.tensor_scalar_mul(out=cs[:, 1, :, 64:128], in0=sn[:, :, 0:64], scalar1=-1.0)
             else:
-                nc.scalar.copy(out=cs[:, 1, ta:tb, 0:64], in_=sn[:, ta:tb, 64:128])
-                nc.scalar.mul(out=cs[:, 1, ta:tb, 64:128], in_=sn[:, ta:tb, 0:64], mul=-1.0)
+                nc.scalar.copy(out=cs[:, 1, :, 0:64], in_=sn[:, :, 64:128])
+                nc.scalar.mul(out=cs[:, 1, :, 64:128], in_=sn[:, :, 0:64], mul=-1.0)
 
         def transpose_pair(src_words, dst_words, on_vector):
             xt = ps_t.tile([P, 512], F32, name="xt")
@@ -187,11 +184,10 @@ def tile_mistralattention_t_kernel(tc, hidden_states, cos, sin, q_w, k_w, v_w, o
         )
         load_x(0, 0, 2)
         load_x(0, 2, 4)
-        load_tables(0, 0, GT)
+        load_tables(0)
         nc.sync.dma_start(out=w_sb[:, 2 * H : 3 * H], in_=k_w)
         nc.sync.dma_start(out=w_sb[:, 3 * H : 4 * H], in_=v_w)
         load_x(0, 4, 8)
-        load_tables(0, GT, BT)
         new_block(1)
         load_x(1, 0, 4)
         load_x(1, 4, 8)
@@ -206,7 +202,7 @@ def tile_mistralattention_t_kernel(tc, hidden_states, cos, sin, q_w, k_w, v_w, o
         new_codes(0)
         quantise(wgrp, wc, ws, 0, 256)
         quantise(grp_of[0], q_of[0][0], q_of[0][1], 0, 256)
-        swap_sin(0, True, 0, GT)
+        swap_sin(0, True)
         quantise(grp_of[0], q_of[0][0], q_of[0][1], 256, 512)
 
         for g in range(NG - 1):
@@ -217,7 +213,6 @@ def tile_mistralattention_t_kernel(tc, hidden_states, cos, sin, q_w, k_w, v_w, o
             head(g, 1)
             if g == 0:
                 prep(1)
-                swap_sin(0, False, GT, BT)
                 quant(1)
             head(g, 2)
             head(g, 3)
@@ -237,8 +232,8 @@ def tile_mistralattention_t_kernel(tc, hidden_states, cos, sin, q_w, k_w, v_w, o
         store(g, "v")
         head(g, 0)
         head(g, 1)
-        head(g, 2)
         combine(nc.vector, g, 0, 2)
         store(g, "q")
+        head(g, 2)
         combine(nc.vector, g, 2, 3)
         store(g, "k")

@@ -34,6 +34,7 @@ def tile_mistralattention_t_kernel(tc, hidden_states, cos, sin, q_w, k_w, v_w, o
         tpool = ctx.enter_context(tc.tile_pool(name="tpool", bufs=8))
         ps_t = ctx.enter_context(tc.psum_pool(name="ps_t", bufs=2))
         ps_y = ctx.enter_context(tc.psum_pool(name="ps_y", bufs=6))
+        ctx.enter_context(tc.manual_schedule())
 
         ident = const.tile([P, P], F32)
         make_identity(nc, ident[:])
@@ -132,7 +133,12 @@ def tile_mistralattention_t_kernel(tc, hidden_states, cos, sin, q_w, k_w, v_w, o
         def store(g, what):
             b, t0 = divmod(g * GT, TPB)
             tt, vo = t_blk[g], v_blk[g]
-            if what == "q":
+            if what == "q0" or what == "q1":
+                h = 0 if what == "q0" else 1
+                nc.sync.dma_start(
+                    out=out_0[b, h].rearrange("(p t) d -> p t d", t=TPB)[:, t0 : t0 + GT, :], in_=tt[:, 0, h, :, :]
+                )
+            elif what == "q":
                 nc.sync.dma_start(
                     out=out_0[b].rearrange("h (p t) d -> p h t d", t=TPB)[:, :, t0 : t0 + GT, :], in_=tt[:, 0, 0:2, :, :]
                 )
@@ -221,9 +227,16 @@ def tile_mistralattention_t_kernel(tc, hidden_states, cos, sin, q_w, k_w, v_w, o
                 quant(g + 2)
             if gi == 0 and n + 1 < NBLK:
                 swap_sin(n + 1, False)
-            combine(nc.gpsimd, g, 0, 3)
-            for what in ("v", "q", "k"):
-                store(g, what)
+            if g < NG - 2:
+                combine(nc.gpsimd, g, 0, 3)
+                for what in ("v", "q", "k"):
+                    store(g, what)
+            else:
+                store(g, "v")
+                combine(nc.gpsimd, g, 0, 2)
+                store(g, "q")
+                combine(nc.gpsimd, g, 2, 3)
+                store(g, "k")
             if gi == GPB - 1 and n + XBUFS < NBLK:
                 load_block(n + XBUFS)
 
@@ -232,8 +245,10 @@ def tile_mistralattention_t_kernel(tc, hidden_states, cos, sin, q_w, k_w, v_w, o
         store(g, "v")
         head(g, 0)
         head(g, 1)
-        combine(nc.vector, g, 0, 2)
-        store(g, "q")
         head(g, 2)
+        combine(nc.vector, g, 0, 1)
+        store(g, "q0")
+        combine(nc.vector, g, 1, 2)
+        store(g, "q1")
         combine(nc.vector, g, 2, 3)
         store(g, "k")

from contextlib import ExitStack

import concourse.mybir as mybir
from concourse.masks import make_identity

F32 = mybir.dt.float32
BF16 = mybir.dt.bfloat16
U32 = mybir.dt.uint32
U8 = mybir.dt.uint8
FP8X4 = mybir.dt.float8_e4m3fn_x4
ALU = mybir.AluOpType

P = 128
B, S, H, HD = 2, 4096, 512, 128
TPB = S // P
GT = 4
BT = 8
NBLK = B * TPB // BT
GPB = BT // GT
NG = NBLK * GPB
XBUFS = 6
FLOPS = 2 * B * S * H * 512


def tile_mistralattention_t_kernel(tc, hidden_states, cos, sin, q_w, k_w, v_w, out_0, out_1, out_2):
    nc = tc.nc
    with ExitStack() as ctx:
        const = ctx.enter_context(tc.tile_pool(name="const", bufs=1))
        xpool = ctx.enter_context(tc.tile_pool(name="xpool", bufs=XBUFS))
        cspool = ctx.enter_context(tc.tile_pool(name="cspool", bufs=XBUFS))
        snpool = ctx.enter_context(tc.tile_pool(name="snpool", bufs=6))
        gpool = ctx.enter_context(tc.tile_pool(name="gpool", bufs=3))
        qpool = ctx.enter_context(tc.tile_pool(name="qpool", bufs=3))
        tpool = ctx.enter_context(tc.tile_pool(name="tpool", bufs=8))
        ps_t = ctx.enter_context(tc.psum_pool(name="ps_t", bufs=2))
        ps_y = ctx.enter_context(tc.psum_pool(name="ps_y", bufs=6))
        ctx.enter_context(tc.manual_schedule())

        ident = const.tile([P, P], F32)
        make_identity(nc, ident[:])

        w_sb = const.tile([P, 4 * H], BF16)
        wgrp = const.tile([P, 4 * H], BF16, align_bytes=64)
        wc = const.tile([P, 4 * P], U32, align_bytes=64)
        ws = const.tile([P, 4 * P], U8, align_bytes=64)

        xs_blk = {}
        cs_blk = {}
        sn_blk = {}

        def new_block(n):
            xs_blk[n] = xpool.tile([P, BT * H], BF16, name="xb")
            cs_blk[n] = cspool.tile([P, 2, BT, HD], BF16, name="cs")
            sn_blk[n] = snpool.tile([P, BT, HD], BF16, name="sn")

        def load_x(n, ta, tb):
            b, t0 = divmod(n * BT, TPB)
            xv = hidden_states[b].rearrange("(p t) k -> p t k", t=TPB)
            nc.sync.dma_start(
                out=xs_blk[n][:, ta * H : tb * H], in_=xv[:, t0 + ta : t0 + tb, :].rearrange("p t k -> p (t k)")
            )

        def load_tables(n):
            b, t0 = divmod(n * BT, TPB)
            nc.sync.dma_start(out=sn_blk[n][:], in_=sin[b].rearrange("(p t) d -> p t d", t=TPB)[:, t0 : t0 + BT, :])
            nc.sync.dma_start(
                out=cs_blk[n][:, 0], in_=cos[b].rearrange("(p t) d -> p t d", t=TPB)[:, t0 : t0 + BT, :]
            )

        def load_block(n):
            new_block(n)
            load_x(n, 0, BT)
            load_tables(n)

        def swap_sin(n, on_vector):
            cs, sn = cs_blk[n], sn_blk[n]
            if on_vector:
                nc.vector.tensor_copy(out=cs[:, 1, :, 0:64], in_=sn[:, :, 64:128])
                nc.vector.tensor_scalar_mul(out=cs[:, 1, :, 64:128], in0=sn[:, :, 0:64], scalar1=-1.0)
            else:
                nc.scalar.copy(out=cs[:, 1, :, 0:64], in_=sn[:, :, 64:128])
                nc.scalar.mul(out=cs[:, 1, :, 64:128], in_=sn[:, :, 0:64], mul=-1.0)

        def transpose_pair(src_words, dst_words, on_vector):
            xt = ps_t.tile([P, 512], F32, name="xt")
            for j in range(4):
                nc.tensor.transpose(xt[:, j * 128 : (j + 1) * 128], src_words[:, j * 128 : (j + 1) * 128], ident[:])
            dst = dst_words.rearrange("p (a r u) -> p a r u", a=2, u=2)
            src = xt[:].rearrange("p (a u r) -> p a r u", a=2, u=2)
            if on_vector:
                nc.vector.tensor_copy(out=dst, in_=src)
            else:
                nc.scalar.copy(out=dst, in_=src)

        def quantise(grp, codes, scales, c0, c1):
            nc.vector.quantize_mx(
                out=codes[:, c0:c1].bitcast(FP8X4), scales=scales[:, c0:c1], in_=grp[:, 4 * c0 : 4 * c1]
            )

        grp_of = {}
        q_of = {}

        def prep_half(g, half):
            n, gi = divmod(g, GPB)
            if half == 0:
                grp_of[g] = gpool.tile([P, GT * H], BF16, name="grp", align_bytes=64)
            xw = xs_blk[n][:].bitcast(F32)
            c = gi * GT * 256 + half * 512
            transpose_pair(xw[:, c : c + 512], grp_of[g][:].bitcast(F32)[:, half * 512 : (half + 1) * 512], False)

        def prep(g):
            prep_half(g, 0)
            prep_half(g, 1)

        def new_codes(g):
            xc = qpool.tile([P, GT * P], U32, name="xc", align_bytes=64)
            xs = qpool.tile([P, GT * P], U8, name="xs", align_bytes=64)
            q_of[g] = (xc, xs)

        def quant(g):
            new_codes(g)
            quantise(grp_of[g], q_of[g][0], q_of[g][1], 0, GT * P)

        t_blk = {}
        v_blk = {}

        def combine(eng, g, h0, h1):
            tt = t_blk[g]
            res = tt[:, 0, h0:h1, :, :].rearrange("p h t (f j) -> p (h t) f j", f=2)
            oth = tt[:, 1, h0:h1, :, :].rearrange("p h t (f j) -> p (h t) f j", f=2)
            eng.tensor_tensor(out=res, in0=res, in1=oth[:, :, ::-1, :], op=ALU.add)

        def store(g, what):
            b, t0 = divmod(g * GT, TPB)
            tt, vo = t_blk[g], v_blk[g]
            if what == "q0" or what == "q1":
                h = 0 if what == "q0" else 1
                nc.sync.dma_start(
                    out=out_0[b, h].rearrange("(p t) d -> p t d", t=TPB)[:, t0 : t0 + GT, :], in_=tt[:, 0, h, :, :]
                )
            elif what == "q":
                nc.sync.dma_start(
                    out=out_0[b].rearrange("h (p t) d -> p h t d", t=TPB)[:, :, t0 : t0 + GT, :], in_=tt[:, 0, 0:2, :, :]
                )
            elif what == "k":
                nc.sync.dma_start(
                    out=out_1[b, 0].rearrange("(p t) d -> p t d", t=TPB)[:, t0 : t0 + GT, :], in_=tt[:, 0, 2, :, :]
                )
            else:
                nc.sync.dma_start(out=out_2[b, 0].rearrange("(p t) d -> p t d", t=TPB)[:, t0 : t0 + GT, :], in_=vo[:])

        def passes(g, hb):
            xc, xs = q_of[g]
            y = ps_y.tile([P, 512], F32, name="y")
            for j in range(GT):
                nc.tensor.matmul_mx(
                    out=y[:, j * P : (j + 1) * P],
                    lhsT=xc[:, j * P : (j + 1) * P].bitcast(FP8X4),
                    lhsT_scale=xs[:, j * P : (j + 1) * P],
                    rhs=wc[:, hb * P : (hb + 1) * P].bitcast(FP8X4),
                    rhs_scale=ws[:, hb * P : (hb + 1) * P],
                    start=True,
                    stop=True,
                )
            return y

        def head(g, hb):
            n, gi = divmod(g, GPB)
            if g not in t_blk:
                t_blk[g] = tpool.tile([P, 2, 3, GT, HD], F32, name="tt")
                v_blk[g] = tpool.tile([P, GT, HD], F32, name="vo")
            tt, vo, cs = t_blk[g], v_blk[g], cs_blk[n]
            t0 = gi * GT
            y = passes(g, hb)
            if hb < 3:
                nc.vector.tensor_tensor(
                    out=tt[:, :, hb, :, :].rearrange("p r t d -> p r (t d)"),
                    in0=y[:].unsqueeze(1).to_broadcast([P, 2, 512]),
                    in1=cs[:, :, t0 : t0 + GT, :].rearrange("p r t d -> p r (t d)"),
                    op=ALU.mult,
                )
            else:
                nc.scalar.copy(out=vo[:].rearrange("p t d -> p (t d)"), in_=y[:])

        ww = w_sb[:].bitcast(F32)
        wgw = wgrp[:].bitcast(F32)
        new_block(0)
        nc.sync.dma_start(
            out=w_sb[:, 0 : 2 * H].rearrange("p (a k) -> p a k", a=2), in_=q_w.rearrange("(a p) k -> p a k", p=P)
        )
        load_x(0, 0, 2)
        load_x(0, 2, 4)
        load_tables(0)
        nc.sync.dma_start(out=w_sb[:, 2 * H : 3 * H], in_=k_w)
        nc.sync.dma_start(out=w_sb[:, 3 * H : 4 * H], in_=v_w)
        load_x(0, 4, 8)
        new_block(1)
        load_x(1, 0, 4)
        load_x(1, 4, 8)
        load_tables(1)
        for n in range(2, XBUFS):
            load_block(n)

        transpose_pair(ww[:, 0:512], wgw[:, 0:512], True)
        prep_half(0, 0)
        prep_half(0, 1)
        transpose_pair(ww[:, 512:1024], wgw[:, 512:1024], False)
        new_codes(0)
        quantise(wgrp, wc, ws, 0, 256)
        quantise(grp_of[0], q_of[0][0], q_of[0][1], 0, 256)
        swap_sin(0, True)
        quantise(grp_of[0], q_of[0][0], q_of[0][1], 256, 512)

        for g in range(NG - 1):
            n, gi = divmod(g, GPB)
            head(g, 0)
            if g == 0:
                quantise(wgrp, wc, ws, 256, 512)
            head(g, 1)
            if g == 0:
                prep(1)
                quant(1)
            head(g, 2)
            head(g, 3)
            if g + 2 < NG:
                prep(g + 2)
                quant(g + 2)
            if gi == 0 and n + 1 < NBLK:
                swap_sin(n + 1, False)
            if g < NG - 2:
                combine(nc.gpsimd, g, 0, 3)
                for what in ("v", "q", "k"):
                    store(g, what)
            else:
                store(g, "v")
                combine(nc.gpsimd, g, 0, 2)
                store(g, "q")
                combine(nc.gpsimd, g, 2, 3)
                store(g, "k")
            if gi == GPB - 1 and n + XBUFS < NBLK:
                load_block(n + XBUFS)

        g = NG - 1
        head(g, 3)
        store(g, "v")
        head(g, 0)
        head(g, 1)
        head(g, 2)
        combine(nc.vector, g, 0, 1)
        store(g, "q0")
        combine(nc.vector, g, 1, 2)
        store(g, "q1")
        combine(nc.vector, g, 2, 3)
        store(g, "k")
